import numpy as np
import ml_dtypes

BF16 = ml_dtypes.bfloat16


def bf(x):
    return np.asarray(x, np.float32).astype(BF16)


def f32(x):
    return np.asarray(x, np.float32)


def f64(x):
    return np.asarray(x).astype(np.float64)


def striped(idx):
    return np.tile(idx.reshape(-1, 16).T, (8, 1))


S, H, N = 4096, 128, 2048


def setup_inputs():
    return {"table": bf(np.random.standard_normal((H, S))), "wq": bf(np.random.standard_normal((H, H)) / np.sqrt(H)), "wk": bf(np.random.standard_normal((H, H)) / np.sqrt(H)), "wv": bf(np.random.standard_normal((H, H)) / np.sqrt(H)), "att_w": bf(np.random.standard_normal((H, H)) / np.sqrt(H)), "att_b": f32(0.1 * np.random.standard_normal((H, 1))), "offs": striped(np.random.permutation(np.tile(np.arange(S), 2))[:N])}


def reference(table, wq, wk, wv, att_w, att_b, offs):
    idx = offs[:16].T.reshape(-1)
    x = f64(table)[:, idx]
    return np.concatenate([f64(wq).T @ x, f64(wk).T @ x, f64(wv).T @ x, f64(att_w).T @ x + f64(att_b)], axis=0)

@@ -1,0 +1,54 @@
+import concourse.mybir as mybir
+
+BF16, F32, U16 = mybir.dt.bfloat16, mybir.dt.float32, mybir.dt.uint16
+IDENTITY = mybir.ActivationFunctionType.Identity
+
+P = 128
+TOKENS = 4096
+N = 2048
+PIECE = 512
+PIECE_COLUMNS = PIECE // 16
+
+FLOPS = 2 * 4 * P * P * N
+
+
+def tile_predictor_kernel(tc, table, wq, wk, wv, att_w, att_b, offs, out):
+    nc = tc.nc
+    with (
+        tc.tile_pool(name="held", bufs=1) as held,
+        tc.tile_pool(name="staging", bufs=8) as staging,
+        tc.psum_pool(name="banks", bufs=8) as banks,
+    ):
+        offsets = held.tile([P, N // 16], U16, name="offsets")
+        nc.sync.dma_start(offsets[:], offs)
+        window = held.tile([P, TOKENS], BF16, name="window")
+        nc.sync.dma_start(window[:], table)
+
+        weights = []
+        for name, source in (("wq", wq), ("wk", wk), ("wv", wv), ("att_w", att_w)):
+            weight = held.tile([P, P], BF16, name=name)
+            nc.scalar.dma_start(weight[:], source)
+            weights.append(weight)
+        bias = held.tile([P, 1], F32, name="bias")
+        nc.scalar.dma_start(bias[:], att_b)
+
+        for piece in range(N // PIECE):
+            picked = window[:].indirect(
+                offsets[:, piece * PIECE_COLUMNS : (piece + 1) * PIECE_COLUMNS]
+            )
+            for projection, weight in enumerate(weights):
+                product = banks.tile([P, PIECE], F32, name="product")
+                nc.tensor.matmul(product[:], weight[:], picked, start=True, stop=True)
+
+                staged = staging.tile([P, PIECE], F32, name="staged")
+                if projection == 3:
+                    nc.scalar.activation(staged[:], product[:], IDENTITY, bias=bias[:, 0:1])
+                elif projection == 1:
+                    nc.scalar.copy(staged[:], product[:])
+                else:
+                    nc.vector.tensor_copy(staged[:], product[:])
+
+                nc.sync.dma_start(
+                    out[projection * P : (projection + 1) * P, piece * PIECE : (piece + 1) * PIECE],
+                    staged[:],
+                )

@@ -9,6 +9,8 @@ N = 2048
 PIECE = 512
 PIECE_COLUMNS = PIECE // 16
 
+WARMING_MATMULS = 8
+
 FLOPS = 2 * 4 * P * P * N
 
 
@@ -17,7 +19,8 @@ def tile_predictor_kernel(tc, table, wq, wk, wv, att_w, att_b, offs, out):
     with (
         tc.tile_pool(name="held", bufs=1) as held,
         tc.tile_pool(name="staging", bufs=8) as staging,
-        tc.psum_pool(name="banks", bufs=8) as banks,
+        tc.psum_pool(name="banks", bufs=7) as banks,
+        tc.psum_pool(name="idle_bank", bufs=1) as idle_bank,
     ):
         offsets = held.tile([P, N // 16], U16, name="offsets")
         nc.sync.dma_start(offsets[:], offs)
@@ -31,6 +34,12 @@ def tile_predictor_kernel(tc, table, wq, wk, wv, att_w, att_b, offs, out):
             weights.append(weight)
         bias = held.tile([P, 1], F32, name="bias")
         nc.scalar.dma_start(bias[:], att_b)
+
+        zeros = held.tile([P, PIECE], BF16, name="zeros")
+        nc.vector.memset(zeros[:], 0.0)
+        unread = idle_bank.tile([P, PIECE], F32, name="unread")
+        for warming in range(WARMING_MATMULS):
+            nc.tensor.matmul(unread[:], zeros[:, 0:P], zeros[:], start=True, stop=True)
 
         for piece in range(N // PIECE):
             picked = window[:].indirect(

@@ -9,7 +9,7 @@ N = 2048
 PIECE = 512
 PIECE_COLUMNS = PIECE // 16
 
-WARMING_MATMULS = 8
+PIECES_A_STORE = 2
 
 FLOPS = 2 * 4 * P * P * N
 
@@ -19,8 +19,7 @@ def tile_predictor_kernel(tc, table, wq, wk, wv, att_w, att_b, offs, out):
     with (
         tc.tile_pool(name="held", bufs=1) as held,
         tc.tile_pool(name="staging", bufs=8) as staging,
-        tc.psum_pool(name="banks", bufs=7) as banks,
-        tc.psum_pool(name="idle_bank", bufs=1) as idle_bank,
+        tc.psum_pool(name="banks", bufs=8) as banks,
     ):
         offsets = held.tile([P, N // 16], U16, name="offsets")
         nc.sync.dma_start(offsets[:], offs)
@@ -35,29 +34,32 @@ def tile_predictor_kernel(tc, table, wq, wk, wv, att_w, att_b, offs, out):
         bias = held.tile([P, 1], F32, name="bias")
         nc.scalar.dma_start(bias[:], att_b)
 
-        zeros = held.tile([P, PIECE], BF16, name="zeros")
-        nc.vector.memset(zeros[:], 0.0)
-        unread = idle_bank.tile([P, PIECE], F32, name="unread")
-        for warming in range(WARMING_MATMULS):
-            nc.tensor.matmul(unread[:], zeros[:, 0:P], zeros[:], start=True, stop=True)
+        for projection, weight in enumerate(weights):
+            for first_piece in range(0, N // PIECE, PIECES_A_STORE):
+                staged = staging.tile([P, PIECES_A_STORE * PIECE], F32, name="staged")
+                for place in range(PIECES_A_STORE):
+                    piece = first_piece + place
+                    picked = window[:].indirect(
+                        offsets[:, piece * PIECE_COLUMNS : (piece + 1) * PIECE_COLUMNS]
+                    )
+                    product = banks.tile([P, PIECE], F32, name="product")
+                    nc.tensor.matmul(product[:], weight[:], picked, start=True, stop=True)
 
-        for piece in range(N // PIECE):
-            picked = window[:].indirect(
-                offsets[:, piece * PIECE_COLUMNS : (piece + 1) * PIECE_COLUMNS]
-            )
-            for projection, weight in enumerate(weights):
-                product = banks.tile([P, PIECE], F32, name="product")
-                nc.tensor.matmul(product[:], weight[:], picked, start=True, stop=True)
-
-                staged = staging.tile([P, PIECE], F32, name="staged")
-                if projection == 3:
-                    nc.scalar.activation(staged[:], product[:], IDENTITY, bias=bias[:, 0:1])
-                elif projection == 1:
-                    nc.scalar.copy(staged[:], product[:])
-                else:
-                    nc.vector.tensor_copy(staged[:], product[:])
+                    target = staged[:, place * PIECE : (place + 1) * PIECE]
+                    with_bias = projection == 3
+                    if piece % 2 == 0 and with_bias:
+                        nc.vector.tensor_scalar_add(target, product[:], bias[:, 0:1])
+                    elif piece % 2 == 0:
+                        nc.vector.tensor_copy(target, product[:])
+                    elif with_bias:
+                        nc.scalar.activation(target, product[:], IDENTITY, bias=bias[:, 0:1])
+                    else:
+                        nc.scalar.copy(target, product[:])
 
                 nc.sync.dma_start(
-                    out[projection * P : (projection + 1) * P, piece * PIECE : (piece + 1) * PIECE],
+                    out[
+                        projection * P : (projection + 1) * P,
+                        first_piece * PIECE : (first_piece + PIECES_A_STORE) * PIECE,
+                    ],
                     staged[:],
                 )

@@ -29,10 +29,11 @@ def tile_predictor_kernel(tc, table, wq, wk, wv, att_w, att_b, offs, out):
         weights = []
         for name, source in (("wq", wq), ("wk", wk), ("wv", wv), ("att_w", att_w)):
             weight = held.tile([P, P], BF16, name=name)
-            nc.scalar.dma_start(weight[:], source)
+            queue = nc.scalar if name == "wq" else nc.sync
+            queue.dma_start(weight[:], source)
             weights.append(weight)
         bias = held.tile([P, 1], F32, name="bias")
-        nc.scalar.dma_start(bias[:], att_b)
+        nc.sync.dma_start(bias[:], att_b)
 
         for projection, weight in enumerate(weights):
             for first_piece in range(0, N // PIECE, PIECES_A_STORE):

@@ -11,6 +11,8 @@ PIECE_COLUMNS = PIECE // 16
 
 PIECES_A_STORE = 2
 
+WARMING_MATMULS = 8
+
 FLOPS = 2 * 4 * P * P * N
 
 
@@ -19,7 +21,8 @@ def tile_predictor_kernel(tc, table, wq, wk, wv, att_w, att_b, offs, out):
     with (
         tc.tile_pool(name="held", bufs=1) as held,
         tc.tile_pool(name="staging", bufs=8) as staging,
-        tc.psum_pool(name="banks", bufs=8) as banks,
+        tc.psum_pool(name="banks", bufs=7) as banks,
+        tc.psum_pool(name="idle_bank", bufs=1) as idle_bank,
     ):
         offsets = held.tile([P, N // 16], U16, name="offsets")
         nc.sync.dma_start(offsets[:], offs)
@@ -29,11 +32,16 @@ def tile_predictor_kernel(tc, table, wq, wk, wv, att_w, att_b, offs, out):
         weights = []
         for name, source in (("wq", wq), ("wk", wk), ("wv", wv), ("att_w", att_w)):
             weight = held.tile([P, P], BF16, name=name)
-            queue = nc.scalar if name == "wq" else nc.sync
-            queue.dma_start(weight[:], source)
+            nc.scalar.dma_start(weight[:], source)
             weights.append(weight)
         bias = held.tile([P, 1], F32, name="bias")
-        nc.sync.dma_start(bias[:], att_b)
+        nc.scalar.dma_start(bias[:], att_b)
+
+        zeros = held.tile([P, PIECE], BF16, name="zeros")
+        nc.vector.memset(zeros[:], 0.0)
+        unread = idle_bank.tile([P, PIECE], F32, name="unread")
+        for warming in range(WARMING_MATMULS):
+            nc.tensor.matmul(unread[:], zeros[:, 0:P], zeros[:], start=True, stop=True)
 
         for projection, weight in enumerate(weights):
             for first_piece in range(0, N // PIECE, PIECES_A_STORE):

@@ -11,8 +11,6 @@ PIECE_COLUMNS = PIECE // 16
 
 PIECES_A_STORE = 2
 
-WARMING_MATMULS = 8
-
 FLOPS = 2 * 4 * P * P * N
 
 
@@ -22,7 +20,6 @@ def tile_predictor_kernel(tc, table, wq, wk, wv, att_w, att_b, offs, out):
         tc.tile_pool(name="held", bufs=1) as held,
         tc.tile_pool(name="staging", bufs=8) as staging,
         tc.psum_pool(name="banks", bufs=7) as banks,
-        tc.psum_pool(name="idle_bank", bufs=1) as idle_bank,
     ):
         offsets = held.tile([P, N // 16], U16, name="offsets")
         nc.sync.dma_start(offsets[:], offs)
@@ -36,12 +33,6 @@ def tile_predictor_kernel(tc, table, wq, wk, wv, att_w, att_b, offs, out):
             weights.append(weight)
         bias = held.tile([P, 1], F32, name="bias")
         nc.scalar.dma_start(bias[:], att_b)
-
-        zeros = held.tile([P, PIECE], BF16, name="zeros")
-        nc.vector.memset(zeros[:], 0.0)
-        unread = idle_bank.tile([P, PIECE], F32, name="unread")
-        for warming in range(WARMING_MATMULS):
-            nc.tensor.matmul(unread[:], zeros[:, 0:P], zeros[:], start=True, stop=True)
 
         for projection, weight in enumerate(weights):
             for first_piece in range(0, N // PIECE, PIECES_A_STORE):

@@ -9,6 +9,8 @@ N = 2048
 PIECE = 512
 PIECE_COLUMNS = PIECE // 16
 
+AXI_TRANSACTION = 256
+
 PIECES_A_STORE = 2
 
 FLOPS = 2 * 4 * P * P * N
@@ -23,7 +25,7 @@ def tile_predictor_kernel(tc, table, wq, wk, wv, att_w, att_b, offs, out):
     ):
         offsets = held.tile([P, N // 16], U16, name="offsets")
         nc.sync.dma_start(offsets[:], offs)
-        window = held.tile([P, TOKENS], BF16, name="window")
+        window = held.tile([P, TOKENS], BF16, name="window", align_bytes=AXI_TRANSACTION)
         nc.sync.dma_start(window[:], table)
 
         weights = []
@@ -36,7 +38,9 @@ def tile_predictor_kernel(tc, table, wq, wk, wv, att_w, att_b, offs, out):
 
         for projection, weight in enumerate(weights):
             for first_piece in range(0, N // PIECE, PIECES_A_STORE):
-                staged = staging.tile([P, PIECES_A_STORE * PIECE], F32, name="staged")
+                staged = staging.tile(
+                    [P, PIECES_A_STORE * PIECE], F32, name="staged", align_bytes=AXI_TRANSACTION
+                )
                 for place in range(PIECES_A_STORE):
                     piece = first_piece + place
                     picked = window[:].indirect(

@@ -23,10 +23,10 @@ def tile_predictor_kernel(tc, table, wq, wk, wv, att_w, att_b, offs, out):
         tc.tile_pool(name="staging", bufs=8) as staging,
         tc.psum_pool(name="banks", bufs=7) as banks,
     ):
-        offsets = held.tile([P, N // 16], U16, name="offsets")
-        nc.sync.dma_start(offsets[:], offs)
         window = held.tile([P, TOKENS], BF16, name="window", align_bytes=AXI_TRANSACTION)
         nc.sync.dma_start(window[:], table)
+        offsets = held.tile([P, N // 16], U16, name="offsets")
+        nc.sync.dma_start(offsets[:], offs)
 
         weights = []
         for name, source in (("wq", wq), ("wk", wk), ("wv", wv), ("att_w", att_w)):

@@ -11,7 +11,7 @@ PIECE_COLUMNS = PIECE // 16
 
 AXI_TRANSACTION = 256
 
-PIECES_A_STORE = 2
+STORES = ((1, 1, 2), (2, 2), (2, 2), (2, 1, 1))
 
 FLOPS = 2 * 4 * P * P * N
 
@@ -20,7 +20,7 @@ def tile_predictor_kernel(tc, table, wq, wk, wv, att_w, att_b, offs, out):
     nc = tc.nc
     with (
         tc.tile_pool(name="held", bufs=1) as held,
-        tc.tile_pool(name="staging", bufs=8) as staging,
+        tc.tile_pool(name="staging", bufs=4) as staging,
         tc.psum_pool(name="banks", bufs=7) as banks,
     ):
         window = held.tile([P, TOKENS], BF16, name="window", align_bytes=AXI_TRANSACTION)
@@ -29,27 +29,31 @@ def tile_predictor_kernel(tc, table, wq, wk, wv, att_w, att_b, offs, out):
         nc.sync.dma_start(offsets[:], offs)
 
         weights = []
-        for name, source in (("wq", wq), ("wk", wk), ("wv", wv), ("att_w", att_w)):
+        for queue, name, source in (
+            (nc.scalar, "wq", wq),
+            (nc.gpsimd, "wk", wk),
+            (nc.gpsimd, "wv", wv),
+            (nc.gpsimd, "att_w", att_w),
+        ):
             weight = held.tile([P, P], BF16, name=name)
-            nc.scalar.dma_start(weight[:], source)
+            queue.dma_start(weight[:], source)
             weights.append(weight)
         bias = held.tile([P, 1], F32, name="bias")
-        nc.scalar.dma_start(bias[:], att_b)
+        nc.gpsimd.dma_start(bias[:], att_b)
 
         for projection, weight in enumerate(weights):
-            for first_piece in range(0, N // PIECE, PIECES_A_STORE):
-                staged = staging.tile(
-                    [P, PIECES_A_STORE * PIECE], F32, name="staged", align_bytes=AXI_TRANSACTION
-                )
-                for place in range(PIECES_A_STORE):
-                    piece = first_piece + place
+            staged = staging.tile([P, N], F32, name="staged", align_bytes=AXI_TRANSACTION)
+            piece = 0
+            for pieces_a_store in STORES[projection]:
+                first_entry = piece * PIECE
+                for turn in range(pieces_a_store):
                     picked = window[:].indirect(
                         offsets[:, piece * PIECE_COLUMNS : (piece + 1) * PIECE_COLUMNS]
                     )
                     product = banks.tile([P, PIECE], F32, name="product")
                     nc.tensor.matmul(product[:], weight[:], picked, start=True, stop=True)
 
-                    target = staged[:, place * PIECE : (place + 1) * PIECE]
+                    target = staged[:, piece * PIECE : (piece + 1) * PIECE]
                     with_bias = projection == 3
                     if piece % 2 == 0 and with_bias:
                         nc.vector.tensor_scalar_add(target, product[:], bias[:, 0:1])
@@ -59,11 +63,7 @@ def tile_predictor_kernel(tc, table, wq, wk, wv, att_w, att_b, offs, out):
                         nc.scalar.activation(target, product[:], IDENTITY, bias=bias[:, 0:1])
                     else:
                         nc.scalar.copy(target, product[:])
+                    piece += 1
 
-                nc.sync.dma_start(
-                    out[
-                        projection * P : (projection + 1) * P,
-                        first_piece * PIECE : (first_piece + PIECES_A_STORE) * PIECE,
-                    ],
-                    staged[:],
-                )
+                entries = slice(first_entry, piece * PIECE)
+                nc.sync.dma_start(out[projection * P : (projection + 1) * P, entries], staged[:, entries])

@@ -11,8 +11,6 @@ PIECE_COLUMNS = PIECE // 16
 
 AXI_TRANSACTION = 256
 
-STORES = ((1, 1, 2), (2, 2), (2, 2), (2, 1, 1))
-
 FLOPS = 2 * 4 * P * P * N
 
 
@@ -29,41 +27,34 @@ def tile_predictor_kernel(tc, table, wq, wk, wv, att_w, att_b, offs, out):
         nc.sync.dma_start(offsets[:], offs)
 
         weights = []
-        for queue, name, source in (
-            (nc.scalar, "wq", wq),
-            (nc.gpsimd, "wk", wk),
-            (nc.gpsimd, "wv", wv),
-            (nc.gpsimd, "att_w", att_w),
-        ):
+        for name, source in (("wq", wq), ("wk", wk), ("wv", wv), ("att_w", att_w)):
             weight = held.tile([P, P], BF16, name=name)
-            queue.dma_start(weight[:], source)
+            nc.scalar.dma_start(weight[:], source)
             weights.append(weight)
         bias = held.tile([P, 1], F32, name="bias")
-        nc.gpsimd.dma_start(bias[:], att_b)
+        nc.scalar.dma_start(bias[:], att_b)
 
+        pieces = N // PIECE
         for projection, weight in enumerate(weights):
             staged = staging.tile([P, N], F32, name="staged", align_bytes=AXI_TRANSACTION)
-            piece = 0
-            for pieces_a_store in STORES[projection]:
-                first_entry = piece * PIECE
-                for turn in range(pieces_a_store):
-                    picked = window[:].indirect(
-                        offsets[:, piece * PIECE_COLUMNS : (piece + 1) * PIECE_COLUMNS]
-                    )
-                    product = banks.tile([P, PIECE], F32, name="product")
-                    nc.tensor.matmul(product[:], weight[:], picked, start=True, stop=True)
+            with_bias = projection == len(weights) - 1
+            for piece in range(pieces):
+                picked = window[:].indirect(
+                    offsets[:, piece * PIECE_COLUMNS : (piece + 1) * PIECE_COLUMNS]
+                )
+                product = banks.tile([P, PIECE], F32, name="product")
+                nc.tensor.matmul(product[:], weight[:], picked, start=True, stop=True)
 
-                    target = staged[:, piece * PIECE : (piece + 1) * PIECE]
-                    with_bias = projection == 3
-                    if piece % 2 == 0 and with_bias:
-                        nc.vector.tensor_scalar_add(target, product[:], bias[:, 0:1])
-                    elif piece % 2 == 0:
-                        nc.vector.tensor_copy(target, product[:])
-                    elif with_bias:
-                        nc.scalar.activation(target, product[:], IDENTITY, bias=bias[:, 0:1])
-                    else:
-                        nc.scalar.copy(target, product[:])
-                    piece += 1
+                entries = slice(piece * PIECE, (piece + 1) * PIECE)
+                if piece % 2 == 0 and with_bias:
+                    nc.vector.tensor_scalar_add(staged[:, entries], product[:], bias[:, 0:1])
+                elif piece % 2 == 0:
+                    nc.vector.tensor_copy(staged[:, entries], product[:])
+                elif with_bias:
+                    nc.scalar.activation(staged[:, entries], product[:], IDENTITY, bias=bias[:, 0:1])
+                else:
+                    nc.scalar.copy(staged[:, entries], product[:])
 
-                entries = slice(first_entry, piece * PIECE)
-                nc.sync.dma_start(out[projection * P : (projection + 1) * P, entries], staged[:, entries])
+                last = with_bias and piece == pieces - 1
+                queue = nc.sync if piece % 2 == 0 or last else nc.gpsimd
+                queue.dma_start(out[projection * P : (projection + 1) * P, entries], staged[:, entries])

@@ -1,7 +1,6 @@
 import concourse.mybir as mybir
 
 BF16, F32, U16 = mybir.dt.bfloat16, mybir.dt.float32, mybir.dt.uint16
-IDENTITY = mybir.ActivationFunctionType.Identity
 
 P = 128
 TOKENS = 4096
@@ -46,15 +45,10 @@ def tile_predictor_kernel(tc, table, wq, wk, wv, att_w, att_b, offs, out):
                 nc.tensor.matmul(product[:], weight[:], picked, start=True, stop=True)
 
                 entries = slice(piece * PIECE, (piece + 1) * PIECE)
-                if piece % 2 == 0 and with_bias:
+                if with_bias:
                     nc.vector.tensor_scalar_add(staged[:, entries], product[:], bias[:, 0:1])
-                elif piece % 2 == 0:
-                    nc.vector.tensor_copy(staged[:, entries], product[:])
-                elif with_bias:
-                    nc.scalar.activation(staged[:, entries], product[:], IDENTITY, bias=bias[:, 0:1])
                 else:
-                    nc.scalar.copy(staged[:, entries], product[:])
+                    nc.vector.tensor_copy(staged[:, entries], product[:])
 
-                last = with_bias and piece == pieces - 1
-                queue = nc.sync if piece % 2 == 0 or last else nc.gpsimd
+                queue = nc.scalar if piece % 2 == 0 else nc.sync
                 queue.dma_start(out[projection * P : (projection + 1) * P, entries], staged[:, entries])

@@ -47,8 +47,10 @@ def tile_predictor_kernel(tc, table, wq, wk, wv, att_w, att_b, offs, out):
                 entries = slice(piece * PIECE, (piece + 1) * PIECE)
                 if with_bias:
                     nc.vector.tensor_scalar_add(staged[:, entries], product[:], bias[:, 0:1])
+                elif piece == 2:
+                    nc.scalar.copy(staged[:, entries], product[:])
                 else:
                     nc.vector.tensor_copy(staged[:, entries], product[:])
 
-                queue = nc.scalar if piece % 2 == 0 else nc.sync
+                queue = nc.scalar if piece == 2 else nc.sync
                 queue.dma_start(out[projection * P : (projection + 1) * P, entries], staged[:, entries])

import concourse.mybir as mybir

BF16, F32, U16 = mybir.dt.bfloat16, mybir.dt.float32, mybir.dt.uint16

P = 128
TOKENS = 4096
N = 2048
PIECE = 512
PIECE_COLUMNS = PIECE // 16

AXI_TRANSACTION = 256

FLOPS = 2 * 4 * P * P * N


def tile_predictor_kernel(tc, table, wq, wk, wv, att_w, att_b, offs, out):
    nc = tc.nc
    with (
        tc.tile_pool(name="held", bufs=1) as held,
        tc.tile_pool(name="staging", bufs=4) as staging,
        tc.psum_pool(name="banks", bufs=7) as banks,
    ):
        window = held.tile([P, TOKENS], BF16, name="window", align_bytes=AXI_TRANSACTION)
        nc.sync.dma_start(window[:], table)
        offsets = held.tile([P, N // 16], U16, name="offsets")
        nc.sync.dma_start(offsets[:], offs)

        weights = []
        for name, source in (("wq", wq), ("wk", wk), ("wv", wv), ("att_w", att_w)):
            weight = held.tile([P, P], BF16, name=name)
            nc.scalar.dma_start(weight[:], source)
            weights.append(weight)
        bias = held.tile([P, 1], F32, name="bias")
        nc.scalar.dma_start(bias[:], att_b)

        pieces = N // PIECE
        for projection, weight in enumerate(weights):
            staged = staging.tile([P, N], F32, name="staged", align_bytes=AXI_TRANSACTION)
            with_bias = projection == len(weights) - 1
            for piece in range(pieces):
                picked = window[:].indirect(
                    offsets[:, piece * PIECE_COLUMNS : (piece + 1) * PIECE_COLUMNS]
                )
                product = banks.tile([P, PIECE], F32, name="product")
                nc.tensor.matmul(product[:], weight[:], picked, start=True, stop=True)

                entries = slice(piece * PIECE, (piece + 1) * PIECE)
                if with_bias:
                    nc.vector.tensor_scalar_add(staged[:, entries], product[:], bias[:, 0:1])
                elif piece == 2:
                    nc.scalar.copy(staged[:, entries], product[:])
                else:
                    nc.vector.tensor_copy(staged[:, entries], product[:])

                queue = nc.scalar if piece == 2 else nc.sync
                queue.dma_start(out[projection * P : (projection + 1) * P, entries], staged[:, entries])
